import numpy as np
import ml_dtypes


def mxq(x, axis, fmt="e4m3"):
    dtype, down = {"e4m3": (ml_dtypes.float8_e4m3fn, 7), "e5m2": (ml_dtypes.float8_e5m2, 14)}[fmt]
    v = np.moveaxis(np.asarray(x, np.float32).astype(ml_dtypes.bfloat16).astype(np.float64), axis, -1)
    blocks = v.reshape(v.shape[:-1] + (-1, 32))
    amax = np.abs(blocks).max(-1, keepdims=True)
    byte = np.maximum(np.where(amax > 0, np.frexp(amax)[1] - 1 + 127, 0) - down, 1)
    scale = np.exp2(byte - 127.0)
    codes = (blocks / scale).astype(np.float32).astype(dtype).astype(np.float64)
    return np.moveaxis((codes * scale).reshape(v.shape), -1, axis)


WIDE = False


def mx_kscale(k):
    if not WIDE:
        return np.ones(k)
    levels = np.array([10, -10, 5, -5, 0])
    a = np.random.permutation(np.resize(levels, k // 512 * 4)).reshape(k // 512, 4)
    idx = np.arange(k)
    return np.exp2(a[idx // 512, idx % 128 // 32])


BF16 = ml_dtypes.bfloat16


def bf(x):
    return np.asarray(x, np.float32).astype(BF16)


def f64(x):
    return np.asarray(x).astype(np.float64)


B, CIN, COUT, H, W, NOFF, PAD = 32, 512, 512, 8, 9, 9, 4


def setup_inputs():
    s = mx_kscale(CIN)
    inp = {"x%d" % i: bf(np.random.standard_normal((B, CIN, H, W)) * s[None, :, None, None]) for i in range(NOFF)}
    inp["weights"] = bf(np.random.standard_normal((NOFF, COUT, CIN)) * 0.6 / np.sqrt(CIN) / s)
    inp["bias"] = bf(np.random.standard_normal((NOFF, COUT)) * 0.4)
    return inp


def reference(x0, x1, x2, x3, x4, x5, x6, x7, x8, weights, bias):
    xs = [x0, x1, x2, x3, x4, x5, x6, x7, x8]
    wq = mxq(f64(weights), 2, "e4m3")
    bs = f64(bias)
    out = np.zeros((B, COUT, H, W))
    for i in range(NOFF):
        d = i - PAD
        lo, hi = max(0, -d), W - max(0, d)
        xq = mxq(np.ascontiguousarray(f64(xs[i])[:, :, :, lo:hi]), 1, "e4m3")
        y = (wq[i] @ xq.reshape(B, CIN, H * (hi - lo))).reshape(B, COUT, H, hi - lo)
        y = y + bs[i][None, :, None, None]
        out[:, :, :, lo + d:hi + d] += y
    return out

@@ -1,0 +1,145 @@
+from contextlib import ExitStack
+
+import concourse.mybir as mybir
+from concourse.masks import make_identity
+
+BF16 = mybir.dt.bfloat16
+F32 = mybir.dt.float32
+I32 = mybir.dt.int32
+U32 = mybir.dt.uint32
+U8 = mybir.dt.uint8
+FP8X4 = mybir.dt.float8_e4m3fn_x4
+ADD = mybir.AluOpType.add
+
+B, CIN, COUT, H, W, NOFF, PAD = 32, 512, 512, 8, 9, 9, 4
+P = 128
+PACK = 4
+assert CIN == P * PACK
+BOARD = H * W
+O_TILES = COUT // P
+
+CHUNK_B = 8
+CHUNKS = B // CHUNK_B
+CHUNK_COLS = CHUNK_B * BOARD
+MAIN_N = 512
+MAIN_B = MAIN_N // BOARD
+LAST_N = 128
+LAST_START = CHUNK_COLS - LAST_N
+VECTOR_B = 4
+
+FLOPS = 2 * COUT * CIN * B * H * sum(W - abs(i - PAD) for i in range(NOFF))
+
+
+def tile_scatterhorizontal_kernel(tc, x0, x1, x2, x3, x4, x5, x6, x7, x8, weights, bias, out):
+    nc = tc.nc
+    xs = [x0, x1, x2, x3, x4, x5, x6, x7, x8]
+    with ExitStack() as ctx:
+        const = ctx.enter_context(tc.tile_pool(name="const", bufs=1))
+        w_stage = ctx.enter_context(tc.tile_pool(name="w_stage", bufs=3))
+        x_stage = ctx.enter_context(tc.tile_pool(name="x_stage", bufs=8))
+        x_quant = ctx.enter_context(tc.tile_pool(name="x_quant", bufs=4))
+        out_stage = ctx.enter_context(tc.tile_pool(name="out_stage", bufs=2))
+        psum = ctx.enter_context(tc.psum_pool(name="psum", bufs=8))
+
+        shifted = []
+        for i in range(NOFF):
+            board = const.tile([P, CHUNK_COLS * PACK], BF16, name="shifted%d" % i, align_bytes=64)
+            nc.vector.memset(board[:].bitcast(I32), 0)
+            shifted.append(board)
+
+        ident = const.tile([P, P], F32)
+        make_identity(nc, ident[:])
+        w_codes = const.tile([P, NOFF, COUT], U32, align_bytes=64)
+        w_scales = const.tile([P, NOFF, COUT], U8, align_bytes=64)
+        for i in range(NOFF):
+            w_raw = w_stage.tile([P, O_TILES * CIN], BF16)
+            nc.sync.dma_start(out=w_raw[:], in_=weights[i].rearrange("(m t) k -> m (t k)", t=O_TILES))
+            w_words = w_raw[:].bitcast(F32).rearrange("m (t q u) -> m t u q", t=O_TILES, u=2)
+            w_grouped = w_stage.tile([P, COUT * PACK], BF16, align_bytes=64)
+            w_grouped_words = w_grouped[:].bitcast(F32).rearrange("q (t m u) -> q t m u", t=O_TILES, u=2)
+            for pair in range(O_TILES // 2):
+                w_t = psum.tile([P, 2, 2, P], F32, tag="bank")
+                for s in range(2):
+                    for u in range(2):
+                        nc.tensor.transpose(w_t[:, s, u, :], w_words[:, 2 * pair + s, u, :], ident[:])
+                nc.scalar.copy(
+                    out=w_grouped_words[:, 2 * pair : 2 * pair + 2, :, :],
+                    in_=w_t[:].rearrange("q s u m -> q s m u"),
+                )
+            nc.vector.quantize_mx(
+                out=w_codes[:, i, :].bitcast(FP8X4), scales=w_scales[:, i, :], in_=w_grouped[:]
+            )
+
+        bias_rows = const.tile([P, NOFF, O_TILES], BF16)
+        nc.sync.dma_start(out=bias_rows[:], in_=bias.rearrange("i (m t) -> m i t", t=O_TILES))
+        bias_board = const.tile([P, O_TILES, W], F32)
+        nc.vector.memset(bias_board[:], 0.0)
+        for i in range(NOFF):
+            d = i - PAD
+            c_lo, c_hi = max(0, d), W - max(0, -d)
+            nc.vector.tensor_tensor(
+                out=bias_board[:, :, c_lo:c_hi],
+                in0=bias_board[:, :, c_lo:c_hi],
+                in1=bias_rows[:, i, :].unsqueeze(2).to_broadcast([P, O_TILES, c_hi - c_lo]),
+                op=ADD,
+            )
+
+        for chunk in range(CHUNKS):
+            b0 = chunk * CHUNK_B
+            main = [psum.tile([P, MAIN_N], F32, tag="bank", name="main%d" % t) for t in range(O_TILES)]
+            last = [psum.tile([P, LAST_N], F32, tag="bank", name="last%d" % t) for t in range(O_TILES)]
+            for i in range(NOFF):
+                d = i - PAD
+                w_lo, w_hi = max(0, -d), W - max(0, d)
+                raw = x_stage.tile([P, CHUNK_B, PACK, H, W], BF16)
+                nc.sync.dma_start(
+                    out=raw[:].rearrange("p b t h w -> p b (t h w)"),
+                    in_=xs[i][b0 : b0 + CHUNK_B].rearrange("b (p t) h w -> p b (t h w)", t=PACK),
+                )
+                src = raw[:].rearrange("p b t h w -> p b h w t")
+                dst = shifted[i][:].rearrange("p (b h c t) -> p b h c t", b=CHUNK_B, h=H, c=W)
+                nc.vector.tensor_copy(
+                    out=dst[:, 0:VECTOR_B, :, w_lo + d : w_hi + d, :], in_=src[:, 0:VECTOR_B, :, w_lo:w_hi, :]
+                )
+                nc.scalar.copy(
+                    out=dst[:, VECTOR_B:CHUNK_B, :, w_lo + d : w_hi + d, :],
+                    in_=src[:, VECTOR_B:CHUNK_B, :, w_lo:w_hi, :],
+                )
+                x_codes = x_quant.tile([P, CHUNK_COLS], U32, align_bytes=64)
+                x_scales = x_quant.tile([P, CHUNK_COLS], U8, align_bytes=64)
+                for lo, hi in ((0, MAIN_N), (MAIN_N, CHUNK_COLS)):
+                    nc.vector.quantize_mx(
+                        out=x_codes[:, lo:hi].bitcast(FP8X4),
+                        scales=x_scales[:, lo:hi],
+                        in_=shifted[i][:, lo * PACK : hi * PACK],
+                    )
+                for t in range(O_TILES):
+                    o_cols = slice(t * P, (t + 1) * P)
+                    for acc, cols in ((main[t], slice(0, MAIN_N)), (last[t], slice(LAST_START, CHUNK_COLS))):
+                        nc.tensor.matmul_mx(
+                            out=acc[:],
+                            lhsT=w_codes[:, i, o_cols].bitcast(FP8X4),
+                            lhsT_scale=w_scales[:, i, o_cols],
+                            rhs=x_codes[:, cols].bitcast(FP8X4),
+                            rhs_scale=x_scales[:, cols],
+                            start=(i == 0),
+                            stop=(i == NOFF - 1),
+                        )
+            result = out_stage.tile([P, CHUNK_B, O_TILES, BOARD], F32)
+            for t in range(O_TILES):
+                nc.vector.tensor_tensor(
+                    out=result[:, 0:MAIN_B, t, :].rearrange("p b (h c) -> p b h c", c=W),
+                    in0=main[t][:, 0 : MAIN_B * BOARD].rearrange("p (b h c) -> p b h c", h=H, c=W),
+                    in1=bias_board[:, t, :].unsqueeze(1).unsqueeze(1).to_broadcast([P, MAIN_B, H, W]),
+                    op=ADD,
+                )
+                nc.vector.tensor_tensor(
+                    out=result[:, MAIN_B, t, :].rearrange("p (h c) -> p h c", c=W),
+                    in0=last[t][:, LAST_N - BOARD : LAST_N].rearrange("p (h c) -> p h c", c=W),
+                    in1=bias_board[:, t, :].unsqueeze(1).to_broadcast([P, H, W]),
+                    op=ADD,
+                )
+            nc.sync.dma_start(
+                out=out[b0 : b0 + CHUNK_B].rearrange("b (m t) h c -> m b (t h c)", t=O_TILES),
+                in_=result[:].rearrange("p b t f -> p b (t f)"),
+            )

@@ -25,6 +25,7 @@ MAIN_N = 512
 MAIN_B = MAIN_N // BOARD
 LAST_N = 128
 LAST_START = CHUNK_COLS - LAST_N
+LOAD_B = 4
 VECTOR_B = 4
 
 FLOPS = 2 * COUT * CIN * B * H * sum(W - abs(i - PAD) for i in range(NOFF))
@@ -92,10 +93,11 @@ def tile_scatterhorizontal_kernel(tc, x0, x1, x2, x3, x4, x5, x6, x7, x8, weight
                 d = i - PAD
                 w_lo, w_hi = max(0, -d), W - max(0, d)
                 raw = x_stage.tile([P, CHUNK_B, PACK, H, W], BF16)
-                nc.sync.dma_start(
-                    out=raw[:].rearrange("p b t h w -> p b (t h w)"),
-                    in_=xs[i][b0 : b0 + CHUNK_B].rearrange("b (p t) h w -> p b (t h w)", t=PACK),
-                )
+                for b in range(0, CHUNK_B, LOAD_B):
+                    nc.sync.dma_start(
+                        out=raw[:, b : b + LOAD_B].rearrange("p b t h w -> p b (t h w)"),
+                        in_=xs[i][b0 + b : b0 + b + LOAD_B].rearrange("b (p t) h w -> p b (t h w)", t=PACK),
+                    )
                 src = raw[:].rearrange("p b t h w -> p b h w t")
                 dst = shifted[i][:].rearrange("p (b h c t) -> p b h c t", b=CHUNK_B, h=H, c=W)
                 nc.vector.tensor_copy(

@@ -18,15 +18,15 @@ assert CIN == P * PACK
 BOARD = H * W
 O_TILES = COUT // P
 
-CHUNK_B = 8
-CHUNKS = B // CHUNK_B
-CHUNK_COLS = CHUNK_B * BOARD
-MAIN_N = 512
-MAIN_B = MAIN_N // BOARD
-LAST_N = 128
-LAST_START = CHUNK_COLS - LAST_N
-LOAD_B = 4
-VECTOR_B = 4
+BANK_N = 512
+BANK_B = BANK_N // BOARD
+BANK_USED = BANK_B * BOARD
+BIG_BANKS = 2
+BIG_B = BIG_BANKS * BANK_B
+CHUNKS = ((0, BIG_B), (BIG_B, BIG_B), (2 * BIG_B, B - 2 * BIG_B))
+SMALL_B = B - 2 * BIG_B
+VECTOR_H = 3
+AHEAD = 5
 
 FLOPS = 2 * COUT * CIN * B * H * sum(W - abs(i - PAD) for i in range(NOFF))
 
@@ -35,27 +35,64 @@ def tile_scatterhorizontal_kernel(tc, x0, x1, x2, x3, x4, x5, x6, x7, x8, weight
     nc = tc.nc
     xs = [x0, x1, x2, x3, x4, x5, x6, x7, x8]
     with ExitStack() as ctx:
+        ctx.enter_context(tc.manual_schedule(engines={mybir.EngineType.SP}))
         const = ctx.enter_context(tc.tile_pool(name="const", bufs=1))
-        w_stage = ctx.enter_context(tc.tile_pool(name="w_stage", bufs=3))
-        x_stage = ctx.enter_context(tc.tile_pool(name="x_stage", bufs=8))
-        x_quant = ctx.enter_context(tc.tile_pool(name="x_quant", bufs=4))
-        out_stage = ctx.enter_context(tc.tile_pool(name="out_stage", bufs=2))
+        w_stage = ctx.enter_context(tc.tile_pool(name="w_stage", bufs=2))
+        nine = ctx.enter_context(tc.tile_pool(name="nine", bufs=NOFF))
+        x_stage = ctx.enter_context(tc.tile_pool(name="x_stage", bufs=AHEAD + 1))
+        x_quant = ctx.enter_context(tc.tile_pool(name="x_quant", bufs=3))
+        out_stage = ctx.enter_context(tc.tile_pool(name="out_stage", bufs=3))
         psum = ctx.enter_context(tc.psum_pool(name="psum", bufs=8))
-
-        shifted = []
-        for i in range(NOFF):
-            board = const.tile([P, CHUNK_COLS * PACK], BF16, name="shifted%d" % i, align_bytes=64)
-            nc.vector.memset(board[:].bitcast(I32), 0)
-            shifted.append(board)
 
         ident = const.tile([P, P], F32)
         make_identity(nc, ident[:])
+
+        w_raws = []
+        for i in range(NOFF):
+            w_raw = nine.tile([P, O_TILES * CIN], BF16, tag="nine", name="w_raw%d" % i)
+            nc.sync.dma_start(out=w_raw[:], in_=weights[i].rearrange("(m t) k -> m (t k)", t=O_TILES))
+            w_raws.append(w_raw)
+        bias_rows = const.tile([P, NOFF, O_TILES], BF16)
+        nc.sync.dma_start(out=bias_rows[:], in_=bias.rearrange("i (m t) -> m i t", t=O_TILES))
+
+        steps = [(chunk, i) for chunk in range(len(CHUNKS)) for i in range(NOFF)]
+        big_steps = 2 * NOFF
+        raws = {}
+
+        def load(n):
+            chunk, i = steps[n]
+            b0, nb = CHUNKS[chunk]
+            if nb == BIG_B:
+                raw = x_stage.tile([P, BIG_B, PACK, H, W], BF16, tag="raw", name="raw%d" % n)
+            else:
+                raw = nine.tile([P, SMALL_B, PACK, H, W], BF16, tag="nine", name="raw%d" % n)
+            for b in range(0, nb, BANK_B):
+                e = min(b + BANK_B, nb)
+                nc.sync.dma_start(
+                    out=raw[:, b:e].rearrange("p b t h w -> p b (t h w)"),
+                    in_=xs[i][b0 + b : b0 + e].rearrange("b (p t) h w -> p b (t h w)", t=PACK),
+                )
+            raws[n] = raw
+
+        for n in range(AHEAD):
+            load(n)
+
+        shifted = []
+        for i in range(NOFF):
+            board = const.tile([P, BIG_BANKS * BANK_N * PACK], BF16, name="shifted%d" % i, align_bytes=64)
+            shifted.append(board)
+            d = i - PAD
+            words = board[:].bitcast(F32).rearrange("p (a x) -> p a x", a=BIG_BANKS)
+            nc.gpsimd.memset(words[:, :, BANK_USED * 2 : BANK_N * 2], 0.0)
+            if d != 0:
+                z_lo, z_hi = (0, d) if d > 0 else (W + d, W)
+                rows = words[:, :, 0 : BANK_USED * 2].rearrange("p a (r c u) -> p a r c u", c=W, u=2)
+                nc.gpsimd.memset(rows[:, :, :, z_lo:z_hi, :], 0.0)
+
         w_codes = const.tile([P, NOFF, COUT], U32, align_bytes=64)
         w_scales = const.tile([P, NOFF, COUT], U8, align_bytes=64)
         for i in range(NOFF):
-            w_raw = w_stage.tile([P, O_TILES * CIN], BF16)
-            nc.sync.dma_start(out=w_raw[:], in_=weights[i].rearrange("(m t) k -> m (t k)", t=O_TILES))
-            w_words = w_raw[:].bitcast(F32).rearrange("m (t q u) -> m t u q", t=O_TILES, u=2)
+            w_words = w_raws[i][:].bitcast(F32).rearrange("m (t q u) -> m t u q", t=O_TILES, u=2)
             w_grouped = w_stage.tile([P, COUT * PACK], BF16, align_bytes=64)
             w_grouped_words = w_grouped[:].bitcast(F32).rearrange("q (t m u) -> q t m u", t=O_TILES, u=2)
             for pair in range(O_TILES // 2):
@@ -71,8 +108,6 @@ def tile_scatterhorizontal_kernel(tc, x0, x1, x2, x3, x4, x5, x6, x7, x8, weight
                 out=w_codes[:, i, :].bitcast(FP8X4), scales=w_scales[:, i, :], in_=w_grouped[:]
             )
 
-        bias_rows = const.tile([P, NOFF, O_TILES], BF16)
-        nc.sync.dma_start(out=bias_rows[:], in_=bias.rearrange("i (m t) -> m i t", t=O_TILES))
         bias_board = const.tile([P, O_TILES, W], F32)
         nc.vector.memset(bias_board[:], 0.0)
         for i in range(NOFF):
@@ -85,63 +120,80 @@ def tile_scatterhorizontal_kernel(tc, x0, x1, x2, x3, x4, x5, x6, x7, x8, weight
                 op=ADD,
             )
 
-        for chunk in range(CHUNKS):
-            b0 = chunk * CHUNK_B
-            main = [psum.tile([P, MAIN_N], F32, tag="bank", name="main%d" % t) for t in range(O_TILES)]
-            last = [psum.tile([P, LAST_N], F32, tag="bank", name="last%d" % t) for t in range(O_TILES)]
-            for i in range(NOFF):
-                d = i - PAD
-                w_lo, w_hi = max(0, -d), W - max(0, d)
-                raw = x_stage.tile([P, CHUNK_B, PACK, H, W], BF16)
-                for b in range(0, CHUNK_B, LOAD_B):
-                    nc.sync.dma_start(
-                        out=raw[:, b : b + LOAD_B].rearrange("p b t h w -> p b (t h w)"),
-                        in_=xs[i][b0 + b : b0 + b + LOAD_B].rearrange("b (p t) h w -> p b (t h w)", t=PACK),
-                    )
-                src = raw[:].rearrange("p b t h w -> p b h w t")
-                dst = shifted[i][:].rearrange("p (b h c t) -> p b h c t", b=CHUNK_B, h=H, c=W)
+        acc = []
+        for n in range(len(steps)):
+            chunk, i = steps[n]
+            b0, nb = CHUNKS[chunk]
+            banks = (nb + BANK_B - 1) // BANK_B
+            if n + AHEAD < big_steps:
+                load(n + AHEAD)
+            elif n + AHEAD == big_steps:
+                for m in range(big_steps, len(steps)):
+                    load(m)
+            if i == 0:
+                acc = [
+                    [psum.tile([P, BANK_N], F32, tag="bank", name="acc%d_%d_%d" % (chunk, k, t)) for t in range(O_TILES)]
+                    for k in range(banks)
+                ]
+            d = i - PAD
+            w_lo, w_hi = max(0, -d), W - max(0, d)
+            raw = raws.pop(n)
+            if nb == BIG_B:
+                src = raw[:].rearrange("p (a b) t h w -> p a b h w t", a=BIG_BANKS)
+                dst = (
+                    shifted[i][:]
+                    .rearrange("p (a x) -> p a x", a=BIG_BANKS)[:, :, 0 : BANK_USED * PACK]
+                    .rearrange("p a (b h c t) -> p a b h c t", b=BANK_B, h=H, c=W)
+                )
                 nc.vector.tensor_copy(
-                    out=dst[:, 0:VECTOR_B, :, w_lo + d : w_hi + d, :], in_=src[:, 0:VECTOR_B, :, w_lo:w_hi, :]
+                    out=dst[:, :, :, 0:VECTOR_H, w_lo + d : w_hi + d, :], in_=src[:, :, :, 0:VECTOR_H, w_lo:w_hi, :]
                 )
                 nc.scalar.copy(
-                    out=dst[:, VECTOR_B:CHUNK_B, :, w_lo + d : w_hi + d, :],
-                    in_=src[:, VECTOR_B:CHUNK_B, :, w_lo:w_hi, :],
+                    out=dst[:, :, :, VECTOR_H:H, w_lo + d : w_hi + d, :], in_=src[:, :, :, VECTOR_H:H, w_lo:w_hi, :]
                 )
-                x_codes = x_quant.tile([P, CHUNK_COLS], U32, align_bytes=64)
-                x_scales = x_quant.tile([P, CHUNK_COLS], U8, align_bytes=64)
-                for lo, hi in ((0, MAIN_N), (MAIN_N, CHUNK_COLS)):
-                    nc.vector.quantize_mx(
-                        out=x_codes[:, lo:hi].bitcast(FP8X4),
-                        scales=x_scales[:, lo:hi],
-                        in_=shifted[i][:, lo * PACK : hi * PACK],
-                    )
+            else:
+                src = raw[:].rearrange("p b t h w -> p b h w t")
+                dst = shifted[i][:, 0 : nb * BOARD * PACK].rearrange("p (b h c t) -> p b h c t", b=nb, h=H, c=W)
+                nc.vector.tensor_copy(
+                    out=dst[:, :, 0:VECTOR_H, w_lo + d : w_hi + d, :], in_=src[:, :, 0:VECTOR_H, w_lo:w_hi, :]
+                )
+                nc.scalar.copy(
+                    out=dst[:, :, VECTOR_H:H, w_lo + d : w_hi + d, :], in_=src[:, :, VECTOR_H:H, w_lo:w_hi, :]
+                )
+            x_codes = x_quant.tile([P, BIG_BANKS * BANK_N], U32, align_bytes=64)
+            x_scales = x_quant.tile([P, BIG_BANKS * BANK_N], U8, align_bytes=64)
+            cols = banks * BANK_N
+            nc.vector.quantize_mx(
+                out=x_codes[:, 0:cols].bitcast(FP8X4),
+                scales=x_scales[:, 0:cols],
+                in_=shifted[i][:, 0 : cols * PACK],
+            )
+            for k in range(banks):
+                k_cols = slice(k * BANK_N, (k + 1) * BANK_N)
                 for t in range(O_TILES):
                     o_cols = slice(t * P, (t + 1) * P)
-                    for acc, cols in ((main[t], slice(0, MAIN_N)), (last[t], slice(LAST_START, CHUNK_COLS))):
-                        nc.tensor.matmul_mx(
-                            out=acc[:],
-                            lhsT=w_codes[:, i, o_cols].bitcast(FP8X4),
-                            lhsT_scale=w_scales[:, i, o_cols],
-                            rhs=x_codes[:, cols].bitcast(FP8X4),
-                            rhs_scale=x_scales[:, cols],
-                            start=(i == 0),
-                            stop=(i == NOFF - 1),
+                    nc.tensor.matmul_mx(
+                        out=acc[k][t][:],
+                        lhsT=w_codes[:, i, o_cols].bitcast(FP8X4),
+                        lhsT_scale=w_scales[:, i, o_cols],
+                        rhs=x_codes[:, k_cols].bitcast(FP8X4),
+                        rhs_scale=x_scales[:, k_cols],
+                        start=(i == 0),
+                        stop=(i == NOFF - 1),
+                    )
+            if i == NOFF - 1:
+                for k in range(banks):
+                    kb = min(BANK_B, nb - k * BANK_B)
+                    result = out_stage.tile([P, BANK_B, O_TILES, BOARD], F32)
+                    for t in range(O_TILES):
+                        nc.vector.tensor_tensor(
+                            out=result[:, 0:kb, t, :].rearrange("p b (h c) -> p b h c", c=W),
+                            in0=acc[k][t][:, 0 : kb * BOARD].rearrange("p (b h c) -> p b h c", h=H, c=W),
+                            in1=bias_board[:, t, :].unsqueeze(1).unsqueeze(1).to_broadcast([P, kb, H, W]),
+                            op=ADD,
                         )
-            result = out_stage.tile([P, CHUNK_B, O_TILES, BOARD], F32)
-            for t in range(O_TILES):
-                nc.vector.tensor_tensor(
-                    out=result[:, 0:MAIN_B, t, :].rearrange("p b (h c) -> p b h c", c=W),
-                    in0=main[t][:, 0 : MAIN_B * BOARD].rearrange("p (b h c) -> p b h c", h=H, c=W),
-                    in1=bias_board[:, t, :].unsqueeze(1).unsqueeze(1).to_broadcast([P, MAIN_B, H, W]),
-                    op=ADD,
-                )
-                nc.vector.tensor_tensor(
-                    out=result[:, MAIN_B, t, :].rearrange("p (h c) -> p h c", c=W),
-                    in0=last[t][:, LAST_N - BOARD : LAST_N].rearrange("p (h c) -> p h c", c=W),
-                    in1=bias_board[:, t, :].unsqueeze(1).to_broadcast([P, H, W]),
-                    op=ADD,
-                )
-            nc.sync.dma_start(
-                out=out[b0 : b0 + CHUNK_B].rearrange("b (m t) h c -> m b (t h c)", t=O_TILES),
-                in_=result[:].rearrange("p b t f -> p b (t f)"),
-            )
+                    s0 = b0 + k * BANK_B
+                    nc.sync.dma_start(
+                        out=out[s0 : s0 + kb].rearrange("b (m t) h c -> m b (t h c)", t=O_TILES),
+                        in_=result[:, 0:kb].rearrange("p b t f -> p b (t f)"),
+                    )

@@ -5,7 +5,6 @@ from concourse.masks import make_identity
 
 BF16 = mybir.dt.bfloat16
 F32 = mybir.dt.float32
-I32 = mybir.dt.int32
 U32 = mybir.dt.uint32
 U8 = mybir.dt.uint8
 FP8X4 = mybir.dt.float8_e4m3fn_x4
@@ -19,84 +18,99 @@ BOARD = H * W
 O_TILES = COUT // P
 
 BANK_N = 512
-BANK_B = BANK_N // BOARD
-BANK_USED = BANK_B * BOARD
-BIG_BANKS = 2
-BIG_B = BIG_BANKS * BANK_B
-CHUNKS = ((0, BIG_B), (BIG_B, BIG_B), (2 * BIG_B, B - 2 * BIG_B))
-SMALL_B = B - 2 * BIG_B
-VECTOR_H = 3
-AHEAD = 5
+CHUNK_B = BANK_N // BOARD
+CHUNK_USED = CHUNK_B * BOARD
+CHUNKS = tuple((b0, min(CHUNK_B, B - b0)) for b0 in range(0, B, CHUNK_B))
+AHEAD = 11
+W_AHEAD = 2
 
 FLOPS = 2 * COUT * CIN * B * H * sum(W - abs(i - PAD) for i in range(NOFF))
+
+
+def vector_share(chunk, nb):
+    return 4 if chunk == 0 else 2
 
 
 def tile_scatterhorizontal_kernel(tc, x0, x1, x2, x3, x4, x5, x6, x7, x8, weights, bias, out):
     nc = tc.nc
     xs = [x0, x1, x2, x3, x4, x5, x6, x7, x8]
     with ExitStack() as ctx:
-        ctx.enter_context(tc.manual_schedule(engines={mybir.EngineType.SP}))
+        ctx.enter_context(tc.manual_schedule(engines={mybir.EngineType.SP, mybir.EngineType.PE}))
         const = ctx.enter_context(tc.tile_pool(name="const", bufs=1))
+        w_load = ctx.enter_context(tc.tile_pool(name="w_load", bufs=NOFF))
         w_stage = ctx.enter_context(tc.tile_pool(name="w_stage", bufs=2))
-        nine = ctx.enter_context(tc.tile_pool(name="nine", bufs=NOFF))
         x_stage = ctx.enter_context(tc.tile_pool(name="x_stage", bufs=AHEAD + 1))
-        x_quant = ctx.enter_context(tc.tile_pool(name="x_quant", bufs=3))
+        x_quant = ctx.enter_context(tc.tile_pool(name="x_quant", bufs=4))
         out_stage = ctx.enter_context(tc.tile_pool(name="out_stage", bufs=3))
-        psum = ctx.enter_context(tc.psum_pool(name="psum", bufs=8))
+        psum_even = ctx.enter_context(tc.psum_pool(name="psum_even", bufs=O_TILES))
+        psum_odd = ctx.enter_context(tc.psum_pool(name="psum_odd", bufs=O_TILES))
 
         ident = const.tile([P, P], F32)
         make_identity(nc, ident[:])
 
-        w_raws = []
-        for i in range(NOFF):
-            w_raw = nine.tile([P, O_TILES * CIN], BF16, tag="nine", name="w_raw%d" % i)
-            nc.sync.dma_start(out=w_raw[:], in_=weights[i].rearrange("(m t) k -> m (t k)", t=O_TILES))
-            w_raws.append(w_raw)
-        bias_rows = const.tile([P, NOFF, O_TILES], BF16)
-        nc.sync.dma_start(out=bias_rows[:], in_=bias.rearrange("i (m t) -> m i t", t=O_TILES))
-
         steps = [(chunk, i) for chunk in range(len(CHUNKS)) for i in range(NOFF)]
-        big_steps = 2 * NOFF
+        w_raws = {}
         raws = {}
 
-        def load(n):
+        def load_w(i):
+            w_raw = w_load.tile([P, O_TILES * CIN], BF16, tag="w_raw", name="w_raw%d" % i)
+            nc.sync.dma_start(out=w_raw[:], in_=weights[i].rearrange("(m t) k -> m (t k)", t=O_TILES))
+            w_raws[i] = w_raw
+
+        def load_x(n):
             chunk, i = steps[n]
             b0, nb = CHUNKS[chunk]
-            if nb == BIG_B:
-                raw = x_stage.tile([P, BIG_B, PACK, H, W], BF16, tag="raw", name="raw%d" % n)
-            else:
-                raw = nine.tile([P, SMALL_B, PACK, H, W], BF16, tag="nine", name="raw%d" % n)
-            for b in range(0, nb, BANK_B):
-                e = min(b + BANK_B, nb)
-                nc.sync.dma_start(
-                    out=raw[:, b:e].rearrange("p b t h w -> p b (t h w)"),
-                    in_=xs[i][b0 + b : b0 + e].rearrange("b (p t) h w -> p b (t h w)", t=PACK),
-                )
+            raw = x_stage.tile([P, CHUNK_B, PACK, H, W], BF16, tag="raw", name="raw%d" % n)
+            nc.sync.dma_start(
+                out=raw[:, 0:nb].rearrange("p b t h w -> p b (t h w)"),
+                in_=xs[i][b0 : b0 + nb].rearrange("b (p t) h w -> p b (t h w)", t=PACK),
+            )
             raws[n] = raw
 
-        for n in range(AHEAD):
-            load(n)
+        for i in range(W_AHEAD):
+            load_w(i)
+        for i in range(NOFF):
+            load_x(i)
+            if i + W_AHEAD < NOFF:
+                load_w(i + W_AHEAD)
+        bias_rows = const.tile([P, NOFF, O_TILES], BF16)
+        nc.sync.dma_start(out=bias_rows[:], in_=bias.rearrange("i (m t) -> m i t", t=O_TILES))
+        for n in range(NOFF, AHEAD):
+            load_x(n)
 
         shifted = []
         for i in range(NOFF):
-            board = const.tile([P, BIG_BANKS * BANK_N * PACK], BF16, name="shifted%d" % i, align_bytes=64)
+            board = const.tile([P, BANK_N * PACK], BF16, name="shifted%d" % i, align_bytes=64)
             shifted.append(board)
             d = i - PAD
-            words = board[:].bitcast(F32).rearrange("p (a x) -> p a x", a=BIG_BANKS)
-            nc.gpsimd.memset(words[:, :, BANK_USED * 2 : BANK_N * 2], 0.0)
+            words = board[:].bitcast(F32)
+            nc.gpsimd.memset(words[:, CHUNK_USED * 2 : BANK_N * 2], 0.0)
             if d != 0:
                 z_lo, z_hi = (0, d) if d > 0 else (W + d, W)
-                rows = words[:, :, 0 : BANK_USED * 2].rearrange("p a (r c u) -> p a r c u", c=W, u=2)
-                nc.gpsimd.memset(rows[:, :, :, z_lo:z_hi, :], 0.0)
+                rows = words[:, 0 : CHUNK_USED * 2].rearrange("p (r c u) -> p r c u", c=W, u=2)
+                nc.gpsimd.memset(rows[:, :, z_lo:z_hi, :], 0.0)
+
+        bias_board = const.tile([P, O_TILES, W], F32)
+        nc.gpsimd.memset(bias_board[:], 0.0)
+        for i in range(NOFF):
+            d = i - PAD
+            c_lo, c_hi = max(0, d), W - max(0, -d)
+            nc.gpsimd.tensor_tensor(
+                out=bias_board[:, :, c_lo:c_hi],
+                in0=bias_board[:, :, c_lo:c_hi],
+                in1=bias_rows[:, i, :].unsqueeze(2).to_broadcast([P, O_TILES, c_hi - c_lo]),
+                op=ADD,
+            )
 
         w_codes = const.tile([P, NOFF, COUT], U32, align_bytes=64)
         w_scales = const.tile([P, NOFF, COUT], U8, align_bytes=64)
-        for i in range(NOFF):
+
+        def prepare_w(i):
             w_words = w_raws[i][:].bitcast(F32).rearrange("m (t q u) -> m t u q", t=O_TILES, u=2)
             w_grouped = w_stage.tile([P, COUT * PACK], BF16, align_bytes=64)
             w_grouped_words = w_grouped[:].bitcast(F32).rearrange("q (t m u) -> q t m u", t=O_TILES, u=2)
             for pair in range(O_TILES // 2):
-                w_t = psum.tile([P, 2, 2, P], F32, tag="bank")
+                w_t = psum_odd.tile([P, 2, 2, P], F32, tag="bank")
                 for s in range(2):
                     for u in range(2):
                         nc.tensor.transpose(w_t[:, s, u, :], w_words[:, 2 * pair + s, u, :], ident[:])
@@ -108,92 +122,57 @@ def tile_scatterhorizontal_kernel(tc, x0, x1, x2, x3, x4, x5, x6, x7, x8, weight
                 out=w_codes[:, i, :].bitcast(FP8X4), scales=w_scales[:, i, :], in_=w_grouped[:]
             )
 
-        bias_board = const.tile([P, O_TILES, W], F32)
-        nc.vector.memset(bias_board[:], 0.0)
-        for i in range(NOFF):
-            d = i - PAD
-            c_lo, c_hi = max(0, d), W - max(0, -d)
-            nc.vector.tensor_tensor(
-                out=bias_board[:, :, c_lo:c_hi],
-                in0=bias_board[:, :, c_lo:c_hi],
-                in1=bias_rows[:, i, :].unsqueeze(2).to_broadcast([P, O_TILES, c_hi - c_lo]),
-                op=ADD,
-            )
+        for i in range(W_AHEAD):
+            prepare_w(i)
 
         acc = []
+        held = []
         for n in range(len(steps)):
             chunk, i = steps[n]
             b0, nb = CHUNKS[chunk]
-            banks = (nb + BANK_B - 1) // BANK_B
-            if n + AHEAD < big_steps:
-                load(n + AHEAD)
-            elif n + AHEAD == big_steps:
-                for m in range(big_steps, len(steps)):
-                    load(m)
+            if n + AHEAD < len(steps):
+                load_x(n + AHEAD)
             if i == 0:
-                acc = [
-                    [psum.tile([P, BANK_N], F32, tag="bank", name="acc%d_%d_%d" % (chunk, k, t)) for t in range(O_TILES)]
-                    for k in range(banks)
-                ]
+                pool = psum_even if chunk % 2 == 0 else psum_odd
+                acc = [pool.tile([P, BANK_N], F32, tag="bank", name="acc%d_%d" % (chunk, t)) for t in range(O_TILES)]
             d = i - PAD
             w_lo, w_hi = max(0, -d), W - max(0, d)
             raw = raws.pop(n)
-            if nb == BIG_B:
-                src = raw[:].rearrange("p (a b) t h w -> p a b h w t", a=BIG_BANKS)
-                dst = (
-                    shifted[i][:]
-                    .rearrange("p (a x) -> p a x", a=BIG_BANKS)[:, :, 0 : BANK_USED * PACK]
-                    .rearrange("p a (b h c t) -> p a b h c t", b=BANK_B, h=H, c=W)
+            src = raw[:].rearrange("p b t h w -> p b h w t")
+            dst = shifted[i][:, 0 : CHUNK_USED * PACK].rearrange("p (b h c t) -> p b h c t", b=CHUNK_B, h=H, c=W)
+            vb = vector_share(chunk, nb)
+            nc.vector.tensor_copy(out=dst[:, 0:vb, :, w_lo + d : w_hi + d, :], in_=src[:, 0:vb, :, w_lo:w_hi, :])
+            nc.scalar.copy(out=dst[:, vb:nb, :, w_lo + d : w_hi + d, :], in_=src[:, vb:nb, :, w_lo:w_hi, :])
+            x_codes = x_quant.tile([P, BANK_N], U32, align_bytes=64)
+            x_scales = x_quant.tile([P, BANK_N], U8, align_bytes=64)
+            nc.vector.quantize_mx(out=x_codes[:].bitcast(FP8X4), scales=x_scales[:], in_=shifted[i][:])
+            for t in range(O_TILES):
+                o_cols = slice(t * P, (t + 1) * P)
+                nc.tensor.matmul_mx(
+                    out=acc[t][:],
+                    lhsT=w_codes[:, i, o_cols].bitcast(FP8X4),
+                    lhsT_scale=w_scales[:, i, o_cols],
+                    rhs=x_codes[:].bitcast(FP8X4),
+                    rhs_scale=x_scales[:],
+                    start=(i == 0),
+                    stop=(i == NOFF - 1),
                 )
-                nc.vector.tensor_copy(
-                    out=dst[:, :, :, 0:VECTOR_H, w_lo + d : w_hi + d, :], in_=src[:, :, :, 0:VECTOR_H, w_lo:w_hi, :]
-                )
-                nc.scalar.copy(
-                    out=dst[:, :, :, VECTOR_H:H, w_lo + d : w_hi + d, :], in_=src[:, :, :, VECTOR_H:H, w_lo:w_hi, :]
-                )
-            else:
-                src = raw[:].rearrange("p b t h w -> p b h w t")
-                dst = shifted[i][:, 0 : nb * BOARD * PACK].rearrange("p (b h c t) -> p b h c t", b=nb, h=H, c=W)
-                nc.vector.tensor_copy(
-                    out=dst[:, :, 0:VECTOR_H, w_lo + d : w_hi + d, :], in_=src[:, :, 0:VECTOR_H, w_lo:w_hi, :]
-                )
-                nc.scalar.copy(
-                    out=dst[:, :, VECTOR_H:H, w_lo + d : w_hi + d, :], in_=src[:, :, VECTOR_H:H, w_lo:w_hi, :]
-                )
-            x_codes = x_quant.tile([P, BIG_BANKS * BANK_N], U32, align_bytes=64)
-            x_scales = x_quant.tile([P, BIG_BANKS * BANK_N], U8, align_bytes=64)
-            cols = banks * BANK_N
-            nc.vector.quantize_mx(
-                out=x_codes[:, 0:cols].bitcast(FP8X4),
-                scales=x_scales[:, 0:cols],
-                in_=shifted[i][:, 0 : cols * PACK],
-            )
-            for k in range(banks):
-                k_cols = slice(k * BANK_N, (k + 1) * BANK_N)
-                for t in range(O_TILES):
-                    o_cols = slice(t * P, (t + 1) * P)
-                    nc.tensor.matmul_mx(
-                        out=acc[k][t][:],
-                        lhsT=w_codes[:, i, o_cols].bitcast(FP8X4),
-                        lhsT_scale=w_scales[:, i, o_cols],
-                        rhs=x_codes[:, k_cols].bitcast(FP8X4),
-                        rhs_scale=x_scales[:, k_cols],
-                        start=(i == 0),
-                        stop=(i == NOFF - 1),
-                    )
+            if chunk == 0 and i + W_AHEAD < NOFF:
+                prepare_w(i + W_AHEAD)
             if i == NOFF - 1:
-                for k in range(banks):
-                    kb = min(BANK_B, nb - k * BANK_B)
-                    result = out_stage.tile([P, BANK_B, O_TILES, BOARD], F32)
-                    for t in range(O_TILES):
-                        nc.vector.tensor_tensor(
-                            out=result[:, 0:kb, t, :].rearrange("p b (h c) -> p b h c", c=W),
-                            in0=acc[k][t][:, 0 : kb * BOARD].rearrange("p (b h c) -> p b h c", h=H, c=W),
-                            in1=bias_board[:, t, :].unsqueeze(1).unsqueeze(1).to_broadcast([P, kb, H, W]),
-                            op=ADD,
-                        )
-                    s0 = b0 + k * BANK_B
-                    nc.sync.dma_start(
-                        out=out[s0 : s0 + kb].rearrange("b (m t) h c -> m b (t h c)", t=O_TILES),
-                        in_=result[:, 0:kb].rearrange("p b t f -> p b (t f)"),
+                result = out_stage.tile([P, CHUNK_B, O_TILES, BOARD], F32)
+                for t in range(O_TILES):
+                    nc.vector.tensor_tensor(
+                        out=result[:, 0:nb, t, :].rearrange("p b (h c) -> p b h c", c=W),
+                        in0=acc[t][:, 0 : nb * BOARD].rearrange("p (b h c) -> p b h c", h=H, c=W),
+                        in1=bias_board[:, t, :].unsqueeze(1).unsqueeze(1).to_broadcast([P, nb, H, W]),
+                        op=ADD,
                     )
+                held.append((b0, nb, result))
+                if chunk != len(CHUNKS) - 3:
+                    for s0, sb, res in held:
+                        nc.sync.dma_start(
+                            out=out[s0 : s0 + sb].rearrange("b (m t) h c -> m b (t h c)", t=O_TILES),
+                            in_=res[:, 0:sb].rearrange("p b t f -> p b (t f)"),
+                        )
+                    held.clear()

@@ -41,7 +41,7 @@ def tile_scatterhorizontal_kernel(tc, x0, x1, x2, x3, x4, x5, x6, x7, x8, weight
         w_stage = ctx.enter_context(tc.tile_pool(name="w_stage", bufs=2))
         x_stage = ctx.enter_context(tc.tile_pool(name="x_stage", bufs=AHEAD + 1))
         x_quant = ctx.enter_context(tc.tile_pool(name="x_quant", bufs=4))
-        out_stage = ctx.enter_context(tc.tile_pool(name="out_stage", bufs=3))
+        out_stage = ctx.enter_context(tc.tile_pool(name="out_stage", bufs=4))
         psum_even = ctx.enter_context(tc.psum_pool(name="psum_even", bufs=O_TILES))
         psum_odd = ctx.enter_context(tc.psum_pool(name="psum_odd", bufs=O_TILES))
 
@@ -67,14 +67,17 @@ def tile_scatterhorizontal_kernel(tc, x0, x1, x2, x3, x4, x5, x6, x7, x8, weight
             )
             raws[n] = raw
 
+        bias_raw = const.tile([P, COUT], BF16)
+        nc.gpsimd.memset(bias_raw[:].bitcast(F32), 0.0)
+
         for i in range(W_AHEAD):
             load_w(i)
         for i in range(NOFF):
             load_x(i)
+            if i == 0:
+                nc.sync.dma_start(out=bias_raw[0:NOFF, :], in_=bias)
             if i + W_AHEAD < NOFF:
                 load_w(i + W_AHEAD)
-        bias_rows = const.tile([P, NOFF, O_TILES], BF16)
-        nc.sync.dma_start(out=bias_rows[:], in_=bias.rearrange("i (m t) -> m i t", t=O_TILES))
         for n in range(NOFF, AHEAD):
             load_x(n)
 
@@ -89,18 +92,6 @@ def tile_scatterhorizontal_kernel(tc, x0, x1, x2, x3, x4, x5, x6, x7, x8, weight
                 z_lo, z_hi = (0, d) if d > 0 else (W + d, W)
                 rows = words[:, 0 : CHUNK_USED * 2].rearrange("p (r c u) -> p r c u", c=W, u=2)
                 nc.gpsimd.memset(rows[:, :, z_lo:z_hi, :], 0.0)
-
-        bias_board = const.tile([P, O_TILES, W], F32)
-        nc.gpsimd.memset(bias_board[:], 0.0)
-        for i in range(NOFF):
-            d = i - PAD
-            c_lo, c_hi = max(0, d), W - max(0, -d)
-            nc.gpsimd.tensor_tensor(
-                out=bias_board[:, :, c_lo:c_hi],
-                in0=bias_board[:, :, c_lo:c_hi],
-                in1=bias_rows[:, i, :].unsqueeze(2).to_broadcast([P, O_TILES, c_hi - c_lo]),
-                op=ADD,
-            )
 
         w_codes = const.tile([P, NOFF, COUT], U32, align_bytes=64)
         w_scales = const.tile([P, NOFF, COUT], U8, align_bytes=64)
@@ -124,6 +115,27 @@ def tile_scatterhorizontal_kernel(tc, x0, x1, x2, x3, x4, x5, x6, x7, x8, weight
 
         for i in range(W_AHEAD):
             prepare_w(i)
+
+        bias_t = psum_odd.tile([P, 2, P], F32, tag="bank")
+        bias_words = bias_raw[:].bitcast(F32).rearrange("i (m u) -> i u m", u=2)
+        for u in range(2):
+            nc.tensor.transpose(bias_t[:, u, :], bias_words[:, u, :], ident[:])
+        bias_turned = const.tile([P, NOFF, 2], F32)
+        nc.vector.tensor_copy(out=bias_turned[:], in_=bias_t[:, :, 0:NOFF].rearrange("m u i -> m i u"))
+        bias_cols = bias_turned[:].rearrange("m i u -> m (i u)").bitcast(BF16).rearrange("m (i t) -> m i t", t=O_TILES)
+
+        bias_board = const.tile([P, O_TILES, W], F32)
+        nc.gpsimd.memset(bias_board[:], 0.0)
+        for i in range(NOFF):
+            d = i - PAD
+            c_lo, c_hi = max(0, d), W - max(0, -d)
+            nc.gpsimd.tensor_tensor(
+                out=bias_board[:, :, c_lo:c_hi],
+                in0=bias_board[:, :, c_lo:c_hi],
+                in1=bias_cols[:, i, :].unsqueeze(2).to_broadcast([P, O_TILES, c_hi - c_lo]),
+                op=ADD,
+            )
+
 
         acc = []
         held = []
@@ -169,7 +181,7 @@ def tile_scatterhorizontal_kernel(tc, x0, x1, x2, x3, x4, x5, x6, x7, x8, weight
                         op=ADD,
                     )
                 held.append((b0, nb, result))
-                if chunk != len(CHUNKS) - 3:
+                if chunk not in (len(CHUNKS) - 4, len(CHUNKS) - 3):
                     for s0, sb, res in held:
                         nc.sync.dma_start(
                             out=out[s0 : s0 + sb].rearrange("b (m t) h c -> m b (t h c)", t=O_TILES),

@@ -41,7 +41,7 @@ def tile_scatterhorizontal_kernel(tc, x0, x1, x2, x3, x4, x5, x6, x7, x8, weight
         w_stage = ctx.enter_context(tc.tile_pool(name="w_stage", bufs=2))
         x_stage = ctx.enter_context(tc.tile_pool(name="x_stage", bufs=AHEAD + 1))
         x_quant = ctx.enter_context(tc.tile_pool(name="x_quant", bufs=4))
-        out_stage = ctx.enter_context(tc.tile_pool(name="out_stage", bufs=4))
+        out_stage = ctx.enter_context(tc.tile_pool(name="out_stage", bufs=len(CHUNKS)))
         psum_even = ctx.enter_context(tc.psum_pool(name="psum_even", bufs=O_TILES))
         psum_odd = ctx.enter_context(tc.psum_pool(name="psum_odd", bufs=O_TILES))
 
@@ -181,7 +181,7 @@ def tile_scatterhorizontal_kernel(tc, x0, x1, x2, x3, x4, x5, x6, x7, x8, weight
                         op=ADD,
                     )
                 held.append((b0, nb, result))
-                if chunk not in (len(CHUNKS) - 4, len(CHUNKS) - 3):
+                if chunk >= len(CHUNKS) - 2:
                     for s0, sb, res in held:
                         nc.sync.dma_start(
                             out=out[s0 : s0 + sb].rearrange("b (m t) h c -> m b (t h c)", t=O_TILES),

@@ -45,6 +45,10 @@ def tile_scatterhorizontal_kernel(tc, x0, x1, x2, x3, x4, x5, x6, x7, x8, weight
         psum_even = ctx.enter_context(tc.psum_pool(name="psum_even", bufs=O_TILES))
         psum_odd = ctx.enter_context(tc.psum_pool(name="psum_odd", bufs=O_TILES))
 
+        warm = const.tile([P, 2], F32)
+        nc.vector.memset(warm[:, 0:1], 0.0)
+        nc.scalar.copy(out=warm[:, 1:2], in_=warm[:, 0:1])
+
         ident = const.tile([P, P], F32)
         make_identity(nc, ident[:])
 

@@ -21,21 +21,27 @@ BANK_N = 512
 CHUNK_B = BANK_N // BOARD
 CHUNK_USED = CHUNK_B * BOARD
 CHUNKS = tuple((b0, min(CHUNK_B, B - b0)) for b0 in range(0, B, CHUNK_B))
+STEPS = tuple((chunk, i) for chunk in range(len(CHUNKS)) for i in range(NOFF))
 AHEAD = 11
-W_AHEAD = 2
 
 FLOPS = 2 * COUT * CIN * B * H * sum(W - abs(i - PAD) for i in range(NOFF))
 
 
-def vector_share(chunk, nb):
-    return 4 if chunk == 0 else 2
+def bank_to_empty(slot):
+    chunk, late = divmod(slot - NOFF - 1, NOFF)
+    return (chunk, late) if 0 <= chunk < len(CHUNKS) - 1 and late < O_TILES else None
+
+
+def vector_share(slot):
+    nb = CHUNKS[STEPS[slot][0]][1]
+    return 2 if bank_to_empty(slot) is not None or nb < CHUNK_B else 4
 
 
 def tile_scatterhorizontal_kernel(tc, x0, x1, x2, x3, x4, x5, x6, x7, x8, weights, bias, out):
     nc = tc.nc
     xs = [x0, x1, x2, x3, x4, x5, x6, x7, x8]
     with ExitStack() as ctx:
-        ctx.enter_context(tc.manual_schedule(engines={mybir.EngineType.SP, mybir.EngineType.PE}))
+        ctx.enter_context(tc.manual_schedule())
         const = ctx.enter_context(tc.tile_pool(name="const", bufs=1))
         w_load = ctx.enter_context(tc.tile_pool(name="w_load", bufs=NOFF))
         w_stage = ctx.enter_context(tc.tile_pool(name="w_stage", bufs=2))
@@ -51,8 +57,9 @@ def tile_scatterhorizontal_kernel(tc, x0, x1, x2, x3, x4, x5, x6, x7, x8, weight
 
         ident = const.tile([P, P], F32)
         make_identity(nc, ident[:])
+        bias_raw = const.tile([P, COUT], BF16)
+        nc.gpsimd.memset(bias_raw[:].bitcast(F32), 0.0)
 
-        steps = [(chunk, i) for chunk in range(len(CHUNKS)) for i in range(NOFF)]
         w_raws = {}
         raws = {}
 
@@ -62,7 +69,7 @@ def tile_scatterhorizontal_kernel(tc, x0, x1, x2, x3, x4, x5, x6, x7, x8, weight
             w_raws[i] = w_raw
 
         def load_x(n):
-            chunk, i = steps[n]
+            chunk, i = STEPS[n]
             b0, nb = CHUNKS[chunk]
             raw = x_stage.tile([P, CHUNK_B, PACK, H, W], BF16, tag="raw", name="raw%d" % n)
             nc.sync.dma_start(
@@ -71,17 +78,14 @@ def tile_scatterhorizontal_kernel(tc, x0, x1, x2, x3, x4, x5, x6, x7, x8, weight
             )
             raws[n] = raw
 
-        bias_raw = const.tile([P, COUT], BF16)
-        nc.gpsimd.memset(bias_raw[:].bitcast(F32), 0.0)
-
-        for i in range(W_AHEAD):
-            load_w(i)
+        load_w(0)
+        load_w(1)
         for i in range(NOFF):
             load_x(i)
             if i == 0:
                 nc.sync.dma_start(out=bias_raw[0:NOFF, :], in_=bias)
-            if i + W_AHEAD < NOFF:
-                load_w(i + W_AHEAD)
+            if i + 2 < NOFF:
+                load_w(i + 2)
         for n in range(NOFF, AHEAD):
             load_x(n)
 
@@ -99,13 +103,14 @@ def tile_scatterhorizontal_kernel(tc, x0, x1, x2, x3, x4, x5, x6, x7, x8, weight
 
         w_codes = const.tile([P, NOFF, COUT], U32, align_bytes=64)
         w_scales = const.tile([P, NOFF, COUT], U8, align_bytes=64)
+        w_groupeds = {}
 
-        def prepare_w(i):
+        def turn_w(i):
             w_words = w_raws[i][:].bitcast(F32).rearrange("m (t q u) -> m t u q", t=O_TILES, u=2)
-            w_grouped = w_stage.tile([P, COUT * PACK], BF16, align_bytes=64)
+            w_grouped = w_stage.tile([P, COUT * PACK], BF16, align_bytes=64, tag="w_grouped", name="w_grouped%d" % i)
             w_grouped_words = w_grouped[:].bitcast(F32).rearrange("q (t m u) -> q t m u", t=O_TILES, u=2)
             for pair in range(O_TILES // 2):
-                w_t = psum_odd.tile([P, 2, 2, P], F32, tag="bank")
+                w_t = psum_odd.tile([P, 2, 2, P], F32, tag="bank", name="w_t%d_%d" % (i, pair))
                 for s in range(2):
                     for u in range(2):
                         nc.tensor.transpose(w_t[:, s, u, :], w_words[:, 2 * pair + s, u, :], ident[:])
@@ -113,59 +118,70 @@ def tile_scatterhorizontal_kernel(tc, x0, x1, x2, x3, x4, x5, x6, x7, x8, weight
                     out=w_grouped_words[:, 2 * pair : 2 * pair + 2, :, :],
                     in_=w_t[:].rearrange("q s u m -> q s m u"),
                 )
+            w_groupeds[i] = w_grouped
+
+        def quantise_w(i):
             nc.vector.quantize_mx(
-                out=w_codes[:, i, :].bitcast(FP8X4), scales=w_scales[:, i, :], in_=w_grouped[:]
+                out=w_codes[:, i, :].bitcast(FP8X4), scales=w_scales[:, i, :], in_=w_groupeds.pop(i)[:]
             )
-
-        for i in range(W_AHEAD):
-            prepare_w(i)
-
-        bias_t = psum_odd.tile([P, 2, P], F32, tag="bank")
-        bias_words = bias_raw[:].bitcast(F32).rearrange("i (m u) -> i u m", u=2)
-        for u in range(2):
-            nc.tensor.transpose(bias_t[:, u, :], bias_words[:, u, :], ident[:])
-        bias_turned = const.tile([P, NOFF, 2], F32)
-        nc.vector.tensor_copy(out=bias_turned[:], in_=bias_t[:, :, 0:NOFF].rearrange("m u i -> m i u"))
-        bias_cols = bias_turned[:].rearrange("m i u -> m (i u)").bitcast(BF16).rearrange("m (i t) -> m i t", t=O_TILES)
 
         bias_board = const.tile([P, O_TILES, W], F32)
-        nc.gpsimd.memset(bias_board[:], 0.0)
-        for i in range(NOFF):
-            d = i - PAD
-            c_lo, c_hi = max(0, d), W - max(0, -d)
-            nc.gpsimd.tensor_tensor(
-                out=bias_board[:, :, c_lo:c_hi],
-                in0=bias_board[:, :, c_lo:c_hi],
-                in1=bias_cols[:, i, :].unsqueeze(2).to_broadcast([P, O_TILES, c_hi - c_lo]),
-                op=ADD,
+
+        def sum_bias():
+            bias_t = psum_odd.tile([P, 2, P], F32, tag="bank", name="bias_t")
+            bias_words = bias_raw[:].bitcast(F32).rearrange("i (m u) -> i u m", u=2)
+            for u in range(2):
+                nc.tensor.transpose(bias_t[:, u, :], bias_words[:, u, :], ident[:])
+            bias_turned = const.tile([P, NOFF, 2], F32)
+            nc.vector.tensor_copy(out=bias_turned[:], in_=bias_t[:, :, 0:NOFF].rearrange("m u i -> m i u"))
+            bias_cols = (
+                bias_turned[:].rearrange("m i u -> m (i u)").bitcast(BF16).rearrange("m (i t) -> m i t", t=O_TILES)
             )
+            nc.gpsimd.memset(bias_board[:], 0.0)
+            for i in range(NOFF):
+                d = i - PAD
+                c_lo, c_hi = max(0, d), W - max(0, -d)
+                nc.gpsimd.tensor_tensor(
+                    out=bias_board[:, :, c_lo:c_hi],
+                    in0=bias_board[:, :, c_lo:c_hi],
+                    in1=bias_cols[:, i, :].unsqueeze(2).to_broadcast([P, O_TILES, c_hi - c_lo]),
+                    op=ADD,
+                )
 
+        accs = {}
+        results = {}
+        quants = {}
 
-        acc = []
-        held = []
-        for n in range(len(steps)):
-            chunk, i = steps[n]
-            b0, nb = CHUNKS[chunk]
-            if n + AHEAD < len(steps):
-                load_x(n + AHEAD)
-            if i == 0:
-                pool = psum_even if chunk % 2 == 0 else psum_odd
-                acc = [pool.tile([P, BANK_N], F32, tag="bank", name="acc%d_%d" % (chunk, t)) for t in range(O_TILES)]
+        def regroup(n):
+            chunk, i = STEPS[n]
+            nb = CHUNKS[chunk][1]
             d = i - PAD
             w_lo, w_hi = max(0, -d), W - max(0, d)
-            raw = raws.pop(n)
-            src = raw[:].rearrange("p b t h w -> p b h w t")
+            src = raws.pop(n)[:].rearrange("p b t h w -> p b h w t")
             dst = shifted[i][:, 0 : CHUNK_USED * PACK].rearrange("p (b h c t) -> p b h c t", b=CHUNK_B, h=H, c=W)
-            vb = vector_share(chunk, nb)
+            vb = vector_share(n)
             nc.vector.tensor_copy(out=dst[:, 0:vb, :, w_lo + d : w_hi + d, :], in_=src[:, 0:vb, :, w_lo:w_hi, :])
             nc.scalar.copy(out=dst[:, vb:nb, :, w_lo + d : w_hi + d, :], in_=src[:, vb:nb, :, w_lo:w_hi, :])
-            x_codes = x_quant.tile([P, BANK_N], U32, align_bytes=64)
-            x_scales = x_quant.tile([P, BANK_N], U8, align_bytes=64)
+
+        def quantise(n):
+            i = STEPS[n][1]
+            x_codes = x_quant.tile([P, BANK_N], U32, align_bytes=64, tag="x_codes", name="x_codes%d" % n)
+            x_scales = x_quant.tile([P, BANK_N], U8, align_bytes=64, tag="x_scales", name="x_scales%d" % n)
             nc.vector.quantize_mx(out=x_codes[:].bitcast(FP8X4), scales=x_scales[:], in_=shifted[i][:])
+            quants[n] = (x_codes, x_scales)
+
+        def multiply(n):
+            chunk, i = STEPS[n]
+            if i == 0:
+                pool = psum_even if chunk % 2 == 0 else psum_odd
+                accs[chunk] = [
+                    pool.tile([P, BANK_N], F32, tag="bank", name="acc%d_%d" % (chunk, t)) for t in range(O_TILES)
+                ]
+            x_codes, x_scales = quants.pop(n)
             for t in range(O_TILES):
                 o_cols = slice(t * P, (t + 1) * P)
                 nc.tensor.matmul_mx(
-                    out=acc[t][:],
+                    out=accs[chunk][t][:],
                     lhsT=w_codes[:, i, o_cols].bitcast(FP8X4),
                     lhsT_scale=w_scales[:, i, o_cols],
                     rhs=x_codes[:].bitcast(FP8X4),
@@ -173,22 +189,41 @@ def tile_scatterhorizontal_kernel(tc, x0, x1, x2, x3, x4, x5, x6, x7, x8, weight
                     start=(i == 0),
                     stop=(i == NOFF - 1),
                 )
-            if chunk == 0 and i + W_AHEAD < NOFF:
-                prepare_w(i + W_AHEAD)
-            if i == NOFF - 1:
-                result = out_stage.tile([P, CHUNK_B, O_TILES, BOARD], F32)
-                for t in range(O_TILES):
-                    nc.vector.tensor_tensor(
-                        out=result[:, 0:nb, t, :].rearrange("p b (h c) -> p b h c", c=W),
-                        in0=acc[t][:, 0 : nb * BOARD].rearrange("p (b h c) -> p b h c", h=H, c=W),
-                        in1=bias_board[:, t, :].unsqueeze(1).unsqueeze(1).to_broadcast([P, nb, H, W]),
-                        op=ADD,
-                    )
-                held.append((b0, nb, result))
-                if chunk >= len(CHUNKS) - 2:
-                    for s0, sb, res in held:
-                        nc.sync.dma_start(
-                            out=out[s0 : s0 + sb].rearrange("b (m t) h c -> m b (t h c)", t=O_TILES),
-                            in_=res[:, 0:sb].rearrange("p b t f -> p b (t f)"),
-                        )
-                    held.clear()
+
+        def empty_bank(chunk, t):
+            nb = CHUNKS[chunk][1]
+            if t == 0:
+                results[chunk] = out_stage.tile([P, CHUNK_B, O_TILES, BOARD], F32, tag="result", name="result%d" % chunk)
+            nc.vector.tensor_tensor(
+                out=results[chunk][:, 0:nb, t, :].rearrange("p b (h c) -> p b h c", c=W),
+                in0=accs[chunk][t][:, 0 : nb * BOARD].rearrange("p (b h c) -> p b h c", h=H, c=W),
+                in1=bias_board[:, t, :].unsqueeze(1).unsqueeze(1).to_broadcast([P, nb, H, W]),
+                op=ADD,
+            )
+
+        turn_w(0)
+        for slot in range(len(STEPS) + 1):
+            if slot + AHEAD < len(STEPS):
+                load_x(slot + AHEAD)
+            if slot < len(STEPS):
+                regroup(slot)
+            if slot + 1 < NOFF:
+                turn_w(slot + 1)
+            if slot >= 1:
+                quantise(slot - 1)
+                multiply(slot - 1)
+            if slot < NOFF:
+                quantise_w(slot)
+            if slot == 2:
+                sum_bias()
+            bank = bank_to_empty(slot)
+            if bank is not None:
+                empty_bank(bank[0], bank[1])
+        for t in range(O_TILES):
+            empty_bank(len(CHUNKS) - 1, t)
+        for chunk in range(len(CHUNKS)):
+            b0, nb = CHUNKS[chunk]
+            nc.sync.dma_start(
+                out=out[b0 : b0 + nb].rearrange("b (m t) h c -> m b (t h c)", t=O_TILES),
+                in_=results[chunk][:, 0:nb].rearrange("p b t f -> p b (t f)"),
+            )

@@ -51,10 +51,6 @@ def tile_scatterhorizontal_kernel(tc, x0, x1, x2, x3, x4, x5, x6, x7, x8, weight
         psum_even = ctx.enter_context(tc.psum_pool(name="psum_even", bufs=O_TILES))
         psum_odd = ctx.enter_context(tc.psum_pool(name="psum_odd", bufs=O_TILES))
 
-        warm = const.tile([P, 2], F32)
-        nc.vector.memset(warm[:, 0:1], 0.0)
-        nc.scalar.copy(out=warm[:, 1:2], in_=warm[:, 0:1])
-
         ident = const.tile([P, P], F32)
         make_identity(nc, ident[:])
         bias_raw = const.tile([P, COUT], BF16)

@@ -22,6 +22,7 @@ CHUNK_B = BANK_N // BOARD
 CHUNK_USED = CHUNK_B * BOARD
 CHUNKS = tuple((b0, min(CHUNK_B, B - b0)) for b0 in range(0, B, CHUNK_B))
 STEPS = tuple((chunk, i) for chunk in range(len(CHUNKS)) for i in range(NOFF))
+ROW_PITCH = 384
 AHEAD = 11
 
 FLOPS = 2 * COUT * CIN * B * H * sum(W - abs(i - PAD) for i in range(NOFF))
@@ -60,16 +61,16 @@ def tile_scatterhorizontal_kernel(tc, x0, x1, x2, x3, x4, x5, x6, x7, x8, weight
         raws = {}
 
         def load_w(i):
-            w_raw = w_load.tile([P, O_TILES * CIN], BF16, tag="w_raw", name="w_raw%d" % i)
+            w_raw = w_load.tile([P, O_TILES * CIN], BF16, tag="w_raw", name="w_raw%d" % i, align_bytes=256)
             nc.sync.dma_start(out=w_raw[:], in_=weights[i].rearrange("(m t) k -> m (t k)", t=O_TILES))
             w_raws[i] = w_raw
 
         def load_x(n):
             chunk, i = STEPS[n]
             b0, nb = CHUNKS[chunk]
-            raw = x_stage.tile([P, CHUNK_B, PACK, H, W], BF16, tag="raw", name="raw%d" % n)
+            raw = x_stage.tile([P, CHUNK_B, ROW_PITCH], BF16, tag="raw", name="raw%d" % n, align_bytes=256)
             nc.sync.dma_start(
-                out=raw[:, 0:nb].rearrange("p b t h w -> p b (t h w)"),
+                out=raw[:, 0:nb, 0 : PACK * BOARD],
                 in_=xs[i][b0 : b0 + nb].rearrange("b (p t) h w -> p b (t h w)", t=PACK),
             )
             raws[n] = raw
@@ -153,7 +154,7 @@ def tile_scatterhorizontal_kernel(tc, x0, x1, x2, x3, x4, x5, x6, x7, x8, weight
             nb = CHUNKS[chunk][1]
             d = i - PAD
             w_lo, w_hi = max(0, -d), W - max(0, d)
-            src = raws.pop(n)[:].rearrange("p b t h w -> p b h w t")
+            src = raws.pop(n)[:, :, 0 : PACK * BOARD].rearrange("p b (t h w) -> p b h w t", t=PACK, h=H)
             dst = shifted[i][:, 0 : CHUNK_USED * PACK].rearrange("p (b h c t) -> p b h c t", b=CHUNK_B, h=H, c=W)
             vb = vector_share(n)
             nc.vector.tensor_copy(out=dst[:, 0:vb, :, w_lo + d : w_hi + d, :], in_=src[:, 0:vb, :, w_lo:w_hi, :])
@@ -189,7 +190,9 @@ def tile_scatterhorizontal_kernel(tc, x0, x1, x2, x3, x4, x5, x6, x7, x8, weight
         def empty_bank(chunk, t):
             nb = CHUNKS[chunk][1]
             if t == 0:
-                results[chunk] = out_stage.tile([P, CHUNK_B, O_TILES, BOARD], F32, tag="result", name="result%d" % chunk)
+                results[chunk] = out_stage.tile(
+                    [P, CHUNK_B, O_TILES, BOARD], F32, tag="result", name="result%d" % chunk, align_bytes=256
+                )
             nc.vector.tensor_tensor(
                 out=results[chunk][:, 0:nb, t, :].rearrange("p b (h c) -> p b h c", c=W),
                 in0=accs[chunk][t][:, 0 : nb * BOARD].rearrange("p (b h c) -> p b h c", h=H, c=W),

from contextlib import ExitStack

import concourse.mybir as mybir
from concourse.masks import make_identity

BF16 = mybir.dt.bfloat16
F32 = mybir.dt.float32
U32 = mybir.dt.uint32
U8 = mybir.dt.uint8
FP8X4 = mybir.dt.float8_e4m3fn_x4
ADD = mybir.AluOpType.add

B, CIN, COUT, H, W, NOFF, PAD = 32, 512, 512, 8, 9, 9, 4
P = 128
PACK = 4
assert CIN == P * PACK
BOARD = H * W
O_TILES = COUT // P

BANK_N = 512
CHUNK_B = BANK_N // BOARD
CHUNK_USED = CHUNK_B * BOARD
CHUNKS = tuple((b0, min(CHUNK_B, B - b0)) for b0 in range(0, B, CHUNK_B))
STEPS = tuple((chunk, i) for chunk in range(len(CHUNKS)) for i in range(NOFF))
ROW_PITCH = 384
AHEAD = 11

FLOPS = 2 * COUT * CIN * B * H * sum(W - abs(i - PAD) for i in range(NOFF))


def bank_to_empty(slot):
    chunk, late = divmod(slot - NOFF - 1, NOFF)
    return (chunk, late) if 0 <= chunk < len(CHUNKS) - 1 and late < O_TILES else None


def vector_share(slot):
    nb = CHUNKS[STEPS[slot][0]][1]
    return 2 if bank_to_empty(slot) is not None or nb < CHUNK_B else 4


def tile_scatterhorizontal_kernel(tc, x0, x1, x2, x3, x4, x5, x6, x7, x8, weights, bias, out):
    nc = tc.nc
    xs = [x0, x1, x2, x3, x4, x5, x6, x7, x8]
    with ExitStack() as ctx:
        ctx.enter_context(tc.manual_schedule())
        const = ctx.enter_context(tc.tile_pool(name="const", bufs=1))
        w_load = ctx.enter_context(tc.tile_pool(name="w_load", bufs=NOFF))
        w_stage = ctx.enter_context(tc.tile_pool(name="w_stage", bufs=2))
        x_stage = ctx.enter_context(tc.tile_pool(name="x_stage", bufs=AHEAD + 1))
        x_quant = ctx.enter_context(tc.tile_pool(name="x_quant", bufs=4))
        out_stage = ctx.enter_context(tc.tile_pool(name="out_stage", bufs=len(CHUNKS)))
        psum_even = ctx.enter_context(tc.psum_pool(name="psum_even", bufs=O_TILES))
        psum_odd = ctx.enter_context(tc.psum_pool(name="psum_odd", bufs=O_TILES))

        ident = const.tile([P, P], F32)
        make_identity(nc, ident[:])
        bias_raw = const.tile([P, COUT], BF16)
        nc.gpsimd.memset(bias_raw[:].bitcast(F32), 0.0)

        w_raws = {}
        raws = {}

        def load_w(i):
            w_raw = w_load.tile([P, O_TILES * CIN], BF16, tag="w_raw", name="w_raw%d" % i, align_bytes=256)
            nc.sync.dma_start(out=w_raw[:], in_=weights[i].rearrange("(m t) k -> m (t k)", t=O_TILES))
            w_raws[i] = w_raw

        def load_x(n):
            chunk, i = STEPS[n]
            b0, nb = CHUNKS[chunk]
            raw = x_stage.tile([P, CHUNK_B, ROW_PITCH], BF16, tag="raw", name="raw%d" % n, align_bytes=256)
            nc.sync.dma_start(
                out=raw[:, 0:nb, 0 : PACK * BOARD],
                in_=xs[i][b0 : b0 + nb].rearrange("b (p t) h w -> p b (t h w)", t=PACK),
            )
            raws[n] = raw

        load_w(0)
        load_w(1)
        for i in range(NOFF):
            load_x(i)
            if i == 0:
                nc.sync.dma_start(out=bias_raw[0:NOFF, :], in_=bias)
            if i + 2 < NOFF:
                load_w(i + 2)
        for n in range(NOFF, AHEAD):
            load_x(n)

        shifted = []
        for i in range(NOFF):
            board = const.tile([P, BANK_N * PACK], BF16, name="shifted%d" % i, align_bytes=64)
            shifted.append(board)
            d = i - PAD
            words = board[:].bitcast(F32)
            nc.gpsimd.memset(words[:, CHUNK_USED * 2 : BANK_N * 2], 0.0)
            if d != 0:
                z_lo, z_hi = (0, d) if d > 0 else (W + d, W)
                rows = words[:, 0 : CHUNK_USED * 2].rearrange("p (r c u) -> p r c u", c=W, u=2)
                nc.gpsimd.memset(rows[:, :, z_lo:z_hi, :], 0.0)

        w_codes = const.tile([P, NOFF, COUT], U32, align_bytes=64)
        w_scales = const.tile([P, NOFF, COUT], U8, align_bytes=64)
        w_groupeds = {}

        def turn_w(i):
            w_words = w_raws[i][:].bitcast(F32).rearrange("m (t q u) -> m t u q", t=O_TILES, u=2)
            w_grouped = w_stage.tile([P, COUT * PACK], BF16, align_bytes=64, tag="w_grouped", name="w_grouped%d" % i)
            w_grouped_words = w_grouped[:].bitcast(F32).rearrange("q (t m u) -> q t m u", t=O_TILES, u=2)
            for pair in range(O_TILES // 2):
                w_t = psum_odd.tile([P, 2, 2, P], F32, tag="bank", name="w_t%d_%d" % (i, pair))
                for s in range(2):
                    for u in range(2):
                        nc.tensor.transpose(w_t[:, s, u, :], w_words[:, 2 * pair + s, u, :], ident[:])
                nc.scalar.copy(
                    out=w_grouped_words[:, 2 * pair : 2 * pair + 2, :, :],
                    in_=w_t[:].rearrange("q s u m -> q s m u"),
                )
            w_groupeds[i] = w_grouped

        def quantise_w(i):
            nc.vector.quantize_mx(
                out=w_codes[:, i, :].bitcast(FP8X4), scales=w_scales[:, i, :], in_=w_groupeds.pop(i)[:]
            )

        bias_board = const.tile([P, O_TILES, W], F32)

        def sum_bias():
            bias_t = psum_odd.tile([P, 2, P], F32, tag="bank", name="bias_t")
            bias_words = bias_raw[:].bitcast(F32).rearrange("i (m u) -> i u m", u=2)
            for u in range(2):
                nc.tensor.transpose(bias_t[:, u, :], bias_words[:, u, :], ident[:])
            bias_turned = const.tile([P, NOFF, 2], F32)
            nc.vector.tensor_copy(out=bias_turned[:], in_=bias_t[:, :, 0:NOFF].rearrange("m u i -> m i u"))
            bias_cols = (
                bias_turned[:].rearrange("m i u -> m (i u)").bitcast(BF16).rearrange("m (i t) -> m i t", t=O_TILES)
            )
            nc.gpsimd.memset(bias_board[:], 0.0)
            for i in range(NOFF):
                d = i - PAD
                c_lo, c_hi = max(0, d), W - max(0, -d)
                nc.gpsimd.tensor_tensor(
                    out=bias_board[:, :, c_lo:c_hi],
                    in0=bias_board[:, :, c_lo:c_hi],
                    in1=bias_cols[:, i, :].unsqueeze(2).to_broadcast([P, O_TILES, c_hi - c_lo]),
                    op=ADD,
                )

        accs = {}
        results = {}
        quants = {}

        def regroup(n):
            chunk, i = STEPS[n]
            nb = CHUNKS[chunk][1]
            d = i - PAD
            w_lo, w_hi = max(0, -d), W - max(0, d)
            src = raws.pop(n)[:, :, 0 : PACK * BOARD].rearrange("p b (t h w) -> p b h w t", t=PACK, h=H)
            dst = shifted[i][:, 0 : CHUNK_USED * PACK].rearrange("p (b h c t) -> p b h c t", b=CHUNK_B, h=H, c=W)
            vb = vector_share(n)
            nc.vector.tensor_copy(out=dst[:, 0:vb, :, w_lo + d : w_hi + d, :], in_=src[:, 0:vb, :, w_lo:w_hi, :])
            nc.scalar.copy(out=dst[:, vb:nb, :, w_lo + d : w_hi + d, :], in_=src[:, vb:nb, :, w_lo:w_hi, :])

        def quantise(n):
            i = STEPS[n][1]
            x_codes = x_quant.tile([P, BANK_N], U32, align_bytes=64, tag="x_codes", name="x_codes%d" % n)
            x_scales = x_quant.tile([P, BANK_N], U8, align_bytes=64, tag="x_scales", name="x_scales%d" % n)
            nc.vector.quantize_mx(out=x_codes[:].bitcast(FP8X4), scales=x_scales[:], in_=shifted[i][:])
            quants[n] = (x_codes, x_scales)

        def multiply(n):
            chunk, i = STEPS[n]
            if i == 0:
                pool = psum_even if chunk % 2 == 0 else psum_odd
                accs[chunk] = [
                    pool.tile([P, BANK_N], F32, tag="bank", name="acc%d_%d" % (chunk, t)) for t in range(O_TILES)
                ]
            x_codes, x_scales = quants.pop(n)
            for t in range(O_TILES):
                o_cols = slice(t * P, (t + 1) * P)
                nc.tensor.matmul_mx(
                    out=accs[chunk][t][:],
                    lhsT=w_codes[:, i, o_cols].bitcast(FP8X4),
                    lhsT_scale=w_scales[:, i, o_cols],
                    rhs=x_codes[:].bitcast(FP8X4),
                    rhs_scale=x_scales[:],
                    start=(i == 0),
                    stop=(i == NOFF - 1),
                )

        def empty_bank(chunk, t):
            nb = CHUNKS[chunk][1]
            if t == 0:
                results[chunk] = out_stage.tile(
                    [P, CHUNK_B, O_TILES, BOARD], F32, tag="result", name="result%d" % chunk, align_bytes=256
                )
            nc.vector.tensor_tensor(
                out=results[chunk][:, 0:nb, t, :].rearrange("p b (h c) -> p b h c", c=W),
                in0=accs[chunk][t][:, 0 : nb * BOARD].rearrange("p (b h c) -> p b h c", h=H, c=W),
                in1=bias_board[:, t, :].unsqueeze(1).unsqueeze(1).to_broadcast([P, nb, H, W]),
                op=ADD,
            )

        turn_w(0)
        for slot in range(len(STEPS) + 1):
            if slot + AHEAD < len(STEPS):
                load_x(slot + AHEAD)
            if slot < len(STEPS):
                regroup(slot)
            if slot + 1 < NOFF:
                turn_w(slot + 1)
            if slot >= 1:
                quantise(slot - 1)
                multiply(slot - 1)
            if slot < NOFF:
                quantise_w(slot)
            if slot == 2:
                sum_bias()
            bank = bank_to_empty(slot)
            if bank is not None:
                empty_bank(bank[0], bank[1])
        for t in range(O_TILES):
            empty_bank(len(CHUNKS) - 1, t)
        for chunk in range(len(CHUNKS)):
            b0, nb = CHUNKS[chunk]
            nc.sync.dma_start(
                out=out[b0 : b0 + nb].rearrange("b (m t) h c -> m b (t h c)", t=O_TILES),
                in_=results[chunk][:, 0:nb].rearrange("p b t f -> p b (t f)"),
            )
